import numpy as np
import ml_dtypes


def mxq(x, axis, fmt="e4m3"):
    dtype, down = {"e4m3": (ml_dtypes.float8_e4m3fn, 7), "e5m2": (ml_dtypes.float8_e5m2, 14)}[fmt]
    v = np.moveaxis(np.asarray(x, np.float32).astype(ml_dtypes.bfloat16).astype(np.float64), axis, -1)
    blocks = v.reshape(v.shape[:-1] + (-1, 32))
    amax = np.abs(blocks).max(-1, keepdims=True)
    byte = np.maximum(np.where(amax > 0, np.frexp(amax)[1] - 1 + 127, 0) - down, 1)
    scale = np.exp2(byte - 127.0)
    codes = (blocks / scale).astype(np.float32).astype(dtype).astype(np.float64)
    return np.moveaxis((codes * scale).reshape(v.shape), -1, axis)


WIDE = False


def mx_kscale(k):
    if not WIDE:
        return np.ones(k)
    levels = np.array([20, -20, 10, -10, 0])
    a = np.random.permutation(np.resize(levels, k // 512 * 4)).reshape(k // 512, 4)
    idx = np.arange(k)
    return np.exp2(a[idx // 512, idx % 128 // 32])


BF16 = ml_dtypes.bfloat16


def bf(x):
    return np.asarray(x, np.float32).astype(BF16)


def f64(x):
    return np.asarray(x).astype(np.float64)


B, S, DIM, H, NOPE, ROPE, VHD, KV_RANK = 2, 256, 1536, 16, 128, 64, 128, 512
QKHD = NOPE + ROPE
HALF = ROPE // 2
T = B * S


def rope(u, cos, sin):
    ur = u.reshape(u.shape[:-1] + (HALF, 2))
    a, b = ur[..., 0], ur[..., 1]
    c = cos[None, :, None, :]
    s = sin[None, :, None, :]
    return np.stack([a * c - b * s, a * s + b * c], axis=-1).reshape(u.shape)


def setup_inputs():
    s = mx_kscale(T).reshape(B, S)
    inv_freq = 1.0 / 10000.0 ** (np.arange(0, ROPE, 2) / ROPE)
    ang = np.arange(S)[:, None] * inv_freq[None, :]
    x = np.random.standard_normal((B, S, DIM)) * s[:, :, None]
    wq_w = np.random.standard_normal((DIM, H * QKHD)) / np.sqrt(DIM)
    wq_b = np.random.standard_normal(H * QKHD) * 0.2
    g = np.random.standard_normal((B, S, H, QKHD)) * np.exp2(np.random.randint(-12, 1, (B, S, 1, 1))) / s[:, :, None, None]
    return {"x": bf(x), "wq_w": bf(wq_w), "wq_b": bf(wq_b),
            "cos": bf(np.cos(ang)), "sin": bf(np.sin(ang)), "grad_out": bf(g)}


def reference(x, wq_w, wq_b, cos, sin, grad_out):
    g = f64(grad_out)
    gq = np.concatenate([g[..., :NOPE], rope(g[..., NOPE:], f64(cos), -f64(sin))], axis=-1)
    gq = gq.reshape(T, H * QKHD)
    xt = f64(x).reshape(T, DIM)
    return mxq(xt, 0, "e4m3").T @ mxq(gq, 0, "e5m2")

@@ -1,0 +1,199 @@
+from contextlib import ExitStack
+
+import concourse.mybir as mybir
+
+BF16 = mybir.dt.bfloat16
+F32 = mybir.dt.float32
+U32 = mybir.dt.uint32
+U8 = mybir.dt.uint8
+E4M3_X4 = mybir.dt.float8_e4m3fn_x4
+E5M2_X4 = mybir.dt.float8_e5m2_x4
+MULT = mybir.AluOpType.mult
+ADD = mybir.AluOpType.add
+
+P = 128
+PACK = 4
+TOKENS = P * PACK
+SEQ = 256
+DIM = 1536
+HEADS = 16
+NOPE = 128
+ROPE = 64
+HALF = ROPE // 2
+HEAD = NOPE + ROPE
+COLS = HEADS * HEAD
+M_TILE = 128
+N_TILE = 512
+ROW_TILES = DIM // M_TILE
+X_CHUNK = 512
+X_CHUNKS_ON_SCALAR = 2
+RUN = 4
+
+GROUP_TILES = (1, 2, 3)
+
+FLOPS = 2 * TOKENS * DIM * COLS
+BYTES = 2 * TOKENS * DIM + 2 * TOKENS * COLS + 2 * 2 * SEQ * HALF + 4 * DIM * COLS
+
+
+def tile_mla_pb_kernel(tc, x, wq_w, wq_b, cos, sin, grad_out, out):
+    nc = tc.nc
+
+    x_rows = x.rearrange("b s d -> (b s) d").rearrange("(p t) d -> p t d", t=PACK)
+    g_rows = grad_out.rearrange("b s h c -> (b s) (h c)").rearrange("(p t) c -> p t c", t=PACK)
+
+    group_first_tile = [sum(GROUP_TILES[:k]) for k in range(len(GROUP_TILES))]
+    head_bounds = [0] + [
+        -(-(first + tiles) * N_TILE // HEAD) for first, tiles in zip(group_first_tile, GROUP_TILES)
+    ]
+    most_heads = max(head_bounds[k + 1] - head_bounds[k] for k in range(len(GROUP_TILES)))
+
+    with ExitStack() as ctx:
+        keep = ctx.enter_context(tc.tile_pool(name="keep", bufs=1))
+        products = ctx.enter_context(tc.tile_pool(name="products", bufs=2))
+        stage = ctx.enter_context(tc.tile_pool(name="stage", bufs=8))
+        psum = ctx.enter_context(tc.psum_pool(name="psum", bufs=8))
+        ctx.enter_context(tc.manual_schedule())
+
+        trig = keep.tile([P, 2, PACK, HALF], BF16, name="trig")
+        for half in range(TOKENS // SEQ):
+            rows = slice(half * (SEQ // PACK), (half + 1) * (SEQ // PACK))
+            nc.sync.dma_start(out=trig[rows, 0], in_=cos.rearrange("(p t) f -> p t f", t=PACK))
+            nc.sync.dma_start(out=trig[rows, 1], in_=sin.rearrange("(p t) f -> p t f", t=PACK))
+
+        raw_g = [
+            keep.tile([P, PACK, (head_bounds[k + 1] - head_bounds[k]) * HEAD], BF16, name="raw_g%d" % k)
+            for k in range(len(GROUP_TILES))
+        ]
+        raw_x = [keep.tile([P, PACK, X_CHUNK], BF16, name="raw_x%d" % c) for c in range(DIM // X_CHUNK)]
+
+        def load_g(k):
+            nc.sync.dma_start(
+                out=raw_g[k][:], in_=g_rows[:, :, head_bounds[k] * HEAD : head_bounds[k + 1] * HEAD]
+            )
+
+        load_g(0)
+        for c in range(DIM // X_CHUNK):
+            nc.sync.dma_start(out=raw_x[c][:], in_=x_rows[:, :, c * X_CHUNK : (c + 1) * X_CHUNK])
+        load_g(1)
+        load_g(2)
+
+        cos_table = keep.tile([P, ROPE, PACK], BF16, name="cos_table")
+        sin_table = keep.tile([P, HALF, 2, PACK], BF16, name="sin_table")
+
+        def build_tables():
+            cos_by_pair = trig[:, 0].rearrange("p t f -> p f t")
+            sin_by_pair = trig[:, 1].rearrange("p t f -> p f t")
+            for e in range(2):
+                nc.vector.tensor_copy(
+                    out=cos_table[:].rearrange("p (f e) t -> p f e t", e=2)[:, :, e, :], in_=cos_by_pair
+                )
+            nc.vector.tensor_copy(out=sin_table[:, :, 0, :], in_=sin_by_pair)
+            nc.vector.tensor_scalar_mul(out=sin_table[:, :, 1, :], in0=sin_by_pair, scalar1=-1.0)
+
+        grouped_x = [
+            keep.tile([P, X_CHUNK, PACK], BF16, name="grouped_x%d" % c, align_bytes=64)
+            for c in range(DIM // X_CHUNK)
+        ]
+        grouped_g = keep.tile([P, COLS, PACK], BF16, name="grouped_g", align_bytes=64)
+        x_codes = keep.tile([P, DIM], U32, name="x_codes", align_bytes=64)
+        x_scales = keep.tile([P, DIM], U8, name="x_scales", align_bytes=64)
+        g_codes = keep.tile([P, COLS], U32, name="g_codes", align_bytes=64)
+        g_scales = keep.tile([P, COLS], U8, name="g_scales", align_bytes=64)
+
+        def regroup_x(c, copy):
+            copy(
+                out=grouped_x[c][:].rearrange("p (w i) t -> p w t i", i=RUN),
+                in_=raw_x[c][:].rearrange("p t (w i) -> p w t i", i=RUN),
+            )
+
+        def quantise_x(c):
+            cols = slice(c * X_CHUNK, (c + 1) * X_CHUNK)
+            nc.vector.quantize_mx(
+                out=x_codes[:, cols].bitcast(E4M3_X4),
+                scales=x_scales[:, cols],
+                in_=grouped_x[c][:].rearrange("p w t -> p (w t)"),
+            )
+
+        def prepare_heads(k):
+            heads = slice(head_bounds[k], head_bounds[k + 1])
+            count = head_bounds[k + 1] - head_bounds[k]
+            raw = raw_g[k][:].rearrange("p t (h c) -> p t h c", c=HEAD)
+            grouped = grouped_g[:].rearrange("p (h c) t -> p h c t", c=HEAD)[:, heads]
+
+            nc.vector.tensor_copy(
+                out=grouped[:, :, 0:NOPE, :].rearrange("p h (w i) t -> p h w t i", i=RUN),
+                in_=raw[:, :, :, 0:NOPE].rearrange("p t h (w i) -> p h w t i", i=RUN),
+            )
+
+            if k == 0:
+                build_tables()
+            rotated = raw[:, :, :, NOPE:HEAD]
+            by_cos = products.tile([P, most_heads, ROPE, PACK], F32, name="by_cos")
+            by_sin = products.tile([P, most_heads, ROPE, PACK], F32, name="by_sin")
+            nc.vector.tensor_tensor(
+                out=by_cos[:, 0:count],
+                in0=rotated.rearrange("p t h c -> p h c t"),
+                in1=cos_table[:].unsqueeze(1).to_broadcast([P, count, ROPE, PACK]),
+                op=MULT,
+            )
+            for e in range(2):
+                nc.vector.tensor_tensor(
+                    out=by_sin[:, 0:count].rearrange("p h (f e) t -> p h f e t", e=2)[:, :, :, e, :],
+                    in0=rotated.rearrange("p t h (f e) -> p h f e t", e=2)[:, :, :, 1 - e, :],
+                    in1=sin_table[:, :, e, :].unsqueeze(1).to_broadcast([P, count, HALF, PACK]),
+                    op=MULT,
+                )
+            nc.vector.tensor_tensor(
+                out=grouped[:, :, NOPE:HEAD, :], in0=by_cos[:, 0:count], in1=by_sin[:, 0:count], op=ADD
+            )
+
+        def quantise_g(n):
+            cols = slice(n * N_TILE, (n + 1) * N_TILE)
+            nc.vector.quantize_mx(
+                out=g_codes[:, cols].bitcast(E5M2_X4),
+                scales=g_scales[:, cols],
+                in_=grouped_g[:, cols, :].rearrange("p w t -> p (w t)"),
+            )
+
+        def prepare_group(k):
+            prepare_heads(k)
+            for n in range(group_first_tile[k], group_first_tile[k] + GROUP_TILES[k]):
+                quantise_g(n)
+
+        for c in range(X_CHUNKS_ON_SCALAR):
+            regroup_x(c, nc.scalar.copy)
+        prepare_heads(0)
+        quantise_g(0)
+        quantise_x(0)
+        for c in range(X_CHUNKS_ON_SCALAR, DIM // X_CHUNK):
+            regroup_x(c, nc.vector.tensor_copy)
+        for c in range(1, DIM // X_CHUNK):
+            quantise_x(c)
+
+        last_group = len(GROUP_TILES) - 1
+        for k in range(len(GROUP_TILES)):
+            if k < last_group:
+                prepare_group(k + 1)
+            first_col = group_first_tile[k] * N_TILE
+            width = GROUP_TILES[k] * N_TILE
+            for m in range(ROW_TILES):
+                m_cols = slice(m * M_TILE, (m + 1) * M_TILE)
+                rows = stage.tile([P, max(GROUP_TILES) * N_TILE], F32, name="rows")
+                for i in range(GROUP_TILES[k]):
+                    n_cols = slice(first_col + i * N_TILE, first_col + (i + 1) * N_TILE)
+                    acc = psum.tile([M_TILE, N_TILE], F32, name="acc")
+                    nc.tensor.matmul_mx(
+                        out=acc[:],
+                        lhsT=x_codes[:, m_cols].bitcast(E4M3_X4),
+                        lhsT_scale=x_scales[:, m_cols],
+                        rhs=g_codes[:, n_cols].bitcast(E5M2_X4),
+                        rhs_scale=g_scales[:, n_cols],
+                        start=True,
+                        stop=True,
+                    )
+                    part = rows[:, i * N_TILE : (i + 1) * N_TILE]
+                    if k == last_group and i % 2 == 1:
+                        nc.vector.tensor_copy(out=part, in_=acc[:])
+                    else:
+                        nc.scalar.copy(out=part, in_=acc[:])
+                nc.sync.dma_start(out=out[m_cols, first_col : first_col + width], in_=rows[:, 0:width])

@@ -25,14 +25,33 @@ COLS = HEADS * HEAD
 M_TILE = 128
 N_TILE = 512
 ROW_TILES = DIM // M_TILE
+COL_TILES = COLS // N_TILE
 X_CHUNK = 512
-X_CHUNKS_ON_SCALAR = 2
 RUN = 4
-
-GROUP_TILES = (1, 2, 3)
 
 FLOPS = 2 * TOKENS * DIM * COLS
 BYTES = 2 * TOKENS * DIM + 2 * TOKENS * COLS + 2 * 2 * SEQ * HALF + 4 * DIM * COLS
+
+G_LOADS = ((0, 512), (512, 1024), (1536, 1536))
+UNITS = (
+    ((0, 3), (0, 2)),
+    ((3, 6), (2, 5)),
+    ((6, 8), (5, 8)),
+    ((8, 11), (8, 10)),
+    ((11, 14), (10, 13)),
+    ((14, 16), (13, 16)),
+)
+SWEEPS = (
+    (0, 12, 0, 1, False),
+    (0, 6, 1, 1, False),
+    (6, 6, 1, 2, False),
+    (0, 6, 2, 2, False),
+    (6, 6, 3, 3, True),
+    (0, 6, 4, 2, True),
+)
+MOST_TILES = 3
+MOST_HEADS = 3
+X_CHUNKS_ON_SCALAR = 2
 
 
 def tile_mla_pb_kernel(tc, x, wq_w, wq_b, cos, sin, grad_out, out):
@@ -40,12 +59,6 @@ def tile_mla_pb_kernel(tc, x, wq_w, wq_b, cos, sin, grad_out, out):
 
     x_rows = x.rearrange("b s d -> (b s) d").rearrange("(p t) d -> p t d", t=PACK)
     g_rows = grad_out.rearrange("b s h c -> (b s) (h c)").rearrange("(p t) c -> p t c", t=PACK)
-
-    group_first_tile = [sum(GROUP_TILES[:k]) for k in range(len(GROUP_TILES))]
-    head_bounds = [0] + [
-        -(-(first + tiles) * N_TILE // HEAD) for first, tiles in zip(group_first_tile, GROUP_TILES)
-    ]
-    most_heads = max(head_bounds[k + 1] - head_bounds[k] for k in range(len(GROUP_TILES)))
 
     with ExitStack() as ctx:
         keep = ctx.enter_context(tc.tile_pool(name="keep", bufs=1))
@@ -61,21 +74,30 @@ def tile_mla_pb_kernel(tc, x, wq_w, wq_b, cos, sin, grad_out, out):
             nc.sync.dma_start(out=trig[rows, 1], in_=sin.rearrange("(p t) f -> p t f", t=PACK))
 
         raw_g = [
-            keep.tile([P, PACK, (head_bounds[k + 1] - head_bounds[k]) * HEAD], BF16, name="raw_g%d" % k)
-            for k in range(len(GROUP_TILES))
+            keep.tile([P, PACK, -(-width // HEAD) * HEAD], BF16, name="raw_g%d" % k)
+            for k, (first, width) in enumerate(G_LOADS)
         ]
-        raw_x = [keep.tile([P, PACK, X_CHUNK], BF16, name="raw_x%d" % c) for c in range(DIM // X_CHUNK)]
+        raw_x0 = keep.tile([P, PACK, X_CHUNK], BF16, name="raw_x0")
+        raw_x1 = keep.tile([P, PACK, DIM - X_CHUNK], BF16, name="raw_x1")
 
         def load_g(k):
-            nc.sync.dma_start(
-                out=raw_g[k][:], in_=g_rows[:, :, head_bounds[k] * HEAD : head_bounds[k + 1] * HEAD]
-            )
+            first, width = G_LOADS[k]
+            nc.sync.dma_start(out=raw_g[k][:, :, 0:width], in_=g_rows[:, :, first : first + width])
 
         load_g(0)
-        for c in range(DIM // X_CHUNK):
-            nc.sync.dma_start(out=raw_x[c][:], in_=x_rows[:, :, c * X_CHUNK : (c + 1) * X_CHUNK])
+        nc.sync.dma_start(out=raw_x0[:], in_=x_rows[:, :, 0:X_CHUNK])
+        nc.sync.dma_start(out=raw_x1[:], in_=x_rows[:, :, X_CHUNK:DIM])
         load_g(1)
         load_g(2)
+
+        def raw_stretch(first_head, heads, offset, width):
+            col = first_head * HEAD + offset
+            k = max(i for i, (first, w) in enumerate(G_LOADS) if first <= col)
+            start = col - G_LOADS[k][0]
+            shift = start % HEAD
+            by_head = raw_g[k][:].rearrange("p t (h c) -> p t h c", c=HEAD)
+            assert shift + width <= HEAD
+            return by_head[:, :, start // HEAD : start // HEAD + heads, shift : shift + width]
 
         cos_table = keep.tile([P, ROPE, PACK], BF16, name="cos_table")
         sin_table = keep.tile([P, HALF, 2, PACK], BF16, name="sin_table")
@@ -101,9 +123,10 @@ def tile_mla_pb_kernel(tc, x, wq_w, wq_b, cos, sin, grad_out, out):
         g_scales = keep.tile([P, COLS], U8, name="g_scales", align_bytes=64)
 
         def regroup_x(c, copy):
+            raw = raw_x0[:] if c == 0 else raw_x1[:, :, (c - 1) * X_CHUNK : c * X_CHUNK]
             copy(
                 out=grouped_x[c][:].rearrange("p (w i) t -> p w t i", i=RUN),
-                in_=raw_x[c][:].rearrange("p t (w i) -> p w t i", i=RUN),
+                in_=raw.rearrange("p t (w i) -> p w t i", i=RUN),
             )
 
         def quantise_x(c):
@@ -114,22 +137,19 @@ def tile_mla_pb_kernel(tc, x, wq_w, wq_b, cos, sin, grad_out, out):
                 in_=grouped_x[c][:].rearrange("p w t -> p (w t)"),
             )
 
-        def prepare_heads(k):
-            heads = slice(head_bounds[k], head_bounds[k + 1])
-            count = head_bounds[k + 1] - head_bounds[k]
-            raw = raw_g[k][:].rearrange("p t (h c) -> p t h c", c=HEAD)
-            grouped = grouped_g[:].rearrange("p (h c) t -> p h c t", c=HEAD)[:, heads]
+        grouped_heads = grouped_g[:].rearrange("p (h c) t -> p h c t", c=HEAD)
 
-            nc.vector.tensor_copy(
-                out=grouped[:, :, 0:NOPE, :].rearrange("p h (w i) t -> p h w t i", i=RUN),
-                in_=raw[:, :, :, 0:NOPE].rearrange("p t h (w i) -> p h w t i", i=RUN),
+        def regroup_nope(lo, hi, copy):
+            copy(
+                out=grouped_heads[:, lo:hi, 0:NOPE, :].rearrange("p h (w i) t -> p h w t i", i=RUN),
+                in_=raw_stretch(lo, hi - lo, 0, NOPE).rearrange("p t h (w i) -> p h w t i", i=RUN),
             )
 
-            if k == 0:
-                build_tables()
-            rotated = raw[:, :, :, NOPE:HEAD]
-            by_cos = products.tile([P, most_heads, ROPE, PACK], F32, name="by_cos")
-            by_sin = products.tile([P, most_heads, ROPE, PACK], F32, name="by_sin")
+        def rotate(lo, hi):
+            count = hi - lo
+            rotated = raw_stretch(lo, count, NOPE, ROPE)
+            by_cos = products.tile([P, MOST_HEADS, ROPE, PACK], F32, name="by_cos")
+            by_sin = products.tile([P, MOST_HEADS, ROPE, PACK], F32, name="by_sin")
             nc.vector.tensor_tensor(
                 out=by_cos[:, 0:count],
                 in0=rotated.rearrange("p t h c -> p h c t"),
@@ -144,7 +164,7 @@ def tile_mla_pb_kernel(tc, x, wq_w, wq_b, cos, sin, grad_out, out):
                     op=MULT,
                 )
             nc.vector.tensor_tensor(
-                out=grouped[:, :, NOPE:HEAD, :], in0=by_cos[:, 0:count], in1=by_sin[:, 0:count], op=ADD
+                out=grouped_heads[:, lo:hi, NOPE:HEAD, :], in0=by_cos[:, 0:count], in1=by_sin[:, 0:count], op=ADD
             )
 
         def quantise_g(n):
@@ -155,31 +175,31 @@ def tile_mla_pb_kernel(tc, x, wq_w, wq_b, cos, sin, grad_out, out):
                 in_=grouped_g[:, cols, :].rearrange("p w t -> p (w t)"),
             )
 
-        def prepare_group(k):
-            prepare_heads(k)
-            for n in range(group_first_tile[k], group_first_tile[k] + GROUP_TILES[k]):
-                quantise_g(n)
+        def prepare_unit(n):
+            (nope_lo, nope_hi), (rope_lo, rope_hi) = UNITS[n]
+            regroup_nope(nope_lo, nope_hi, nc.vector.tensor_copy)
+            rotate(rope_lo, rope_hi)
+            quantise_g(n)
 
         for c in range(X_CHUNKS_ON_SCALAR):
             regroup_x(c, nc.scalar.copy)
-        prepare_heads(0)
-        quantise_g(0)
+        build_tables()
+        prepare_unit(0)
         quantise_x(0)
         for c in range(X_CHUNKS_ON_SCALAR, DIM // X_CHUNK):
             regroup_x(c, nc.vector.tensor_copy)
         for c in range(1, DIM // X_CHUNK):
             quantise_x(c)
+        for n in range(1, COL_TILES):
+            prepare_unit(n)
 
-        last_group = len(GROUP_TILES) - 1
-        for k in range(len(GROUP_TILES)):
-            if k < last_group:
-                prepare_group(k + 1)
-            first_col = group_first_tile[k] * N_TILE
-            width = GROUP_TILES[k] * N_TILE
-            for m in range(ROW_TILES):
+        for first_m, count_m, first_n, count_n, vector_too in SWEEPS:
+            first_col = first_n * N_TILE
+            width = count_n * N_TILE
+            for m in range(first_m, first_m + count_m):
                 m_cols = slice(m * M_TILE, (m + 1) * M_TILE)
-                rows = stage.tile([P, max(GROUP_TILES) * N_TILE], F32, name="rows")
-                for i in range(GROUP_TILES[k]):
+                rows = stage.tile([P, MOST_TILES * N_TILE], F32, name="rows")
+                for i in range(count_n):
                     n_cols = slice(first_col + i * N_TILE, first_col + (i + 1) * N_TILE)
                     acc = psum.tile([M_TILE, N_TILE], F32, name="acc")
                     nc.tensor.matmul_mx(
@@ -192,7 +212,7 @@ def tile_mla_pb_kernel(tc, x, wq_w, wq_b, cos, sin, grad_out, out):
                         stop=True,
                     )
                     part = rows[:, i * N_TILE : (i + 1) * N_TILE]
-                    if k == last_group and i % 2 == 1:
+                    if vector_too and i % 2 == 1:
                         nc.vector.tensor_copy(out=part, in_=acc[:])
                     else:
                         nc.scalar.copy(out=part, in_=acc[:])

@@ -145,26 +145,37 @@ def tile_mla_pb_kernel(tc, x, wq_w, wq_b, cos, sin, grad_out, out):
                 in_=raw_stretch(lo, hi - lo, 0, NOPE).rearrange("p t h (w i) -> p h w t i", i=RUN),
             )
 
-        def rotate(lo, hi):
-            count = hi - lo
-            rotated = raw_stretch(lo, count, NOPE, ROPE)
-            by_cos = products.tile([P, MOST_HEADS, ROPE, PACK], F32, name="by_cos")
-            by_sin = products.tile([P, MOST_HEADS, ROPE, PACK], F32, name="by_sin")
+        by_cos = {}
+        by_sin = {}
+
+        def times_sin(n, e):
+            lo, hi = UNITS[n][1]
+            if e == 0:
+                by_sin[n] = products.tile([P, MOST_HEADS, ROPE, PACK], F32, name="by_sin")
             nc.vector.tensor_tensor(
-                out=by_cos[:, 0:count],
-                in0=rotated.rearrange("p t h c -> p h c t"),
-                in1=cos_table[:].unsqueeze(1).to_broadcast([P, count, ROPE, PACK]),
+                out=by_sin[n][:, 0 : hi - lo].rearrange("p h (f e) t -> p h f e t", e=2)[:, :, :, e, :],
+                in0=raw_stretch(lo, hi - lo, NOPE, ROPE).rearrange("p t h (f e) -> p h f e t", e=2)[:, :, :, 1 - e, :],
+                in1=sin_table[:, :, e, :].unsqueeze(1).to_broadcast([P, hi - lo, HALF, PACK]),
                 op=MULT,
             )
-            for e in range(2):
-                nc.vector.tensor_tensor(
-                    out=by_sin[:, 0:count].rearrange("p h (f e) t -> p h f e t", e=2)[:, :, :, e, :],
-                    in0=rotated.rearrange("p t h (f e) -> p h f e t", e=2)[:, :, :, 1 - e, :],
-                    in1=sin_table[:, :, e, :].unsqueeze(1).to_broadcast([P, count, HALF, PACK]),
-                    op=MULT,
-                )
+
+        def times_cos(n):
+            lo, hi = UNITS[n][1]
+            by_cos[n] = products.tile([P, MOST_HEADS, ROPE, PACK], F32, name="by_cos")
             nc.vector.tensor_tensor(
-                out=grouped_heads[:, lo:hi, NOPE:HEAD, :], in0=by_cos[:, 0:count], in1=by_sin[:, 0:count], op=ADD
+                out=by_cos[n][:, 0 : hi - lo],
+                in0=raw_stretch(lo, hi - lo, NOPE, ROPE).rearrange("p t h c -> p h c t"),
+                in1=cos_table[:].unsqueeze(1).to_broadcast([P, hi - lo, ROPE, PACK]),
+                op=MULT,
+            )
+
+        def add_products(n):
+            lo, hi = UNITS[n][1]
+            nc.vector.tensor_tensor(
+                out=grouped_heads[:, lo:hi, NOPE:HEAD, :],
+                in0=by_cos[n][:, 0 : hi - lo],
+                in1=by_sin[n][:, 0 : hi - lo],
+                op=ADD,
             )
 
         def quantise_g(n):
@@ -175,23 +186,29 @@ def tile_mla_pb_kernel(tc, x, wq_w, wq_b, cos, sin, grad_out, out):
                 in_=grouped_g[:, cols, :].rearrange("p w t -> p (w t)"),
             )
 
-        def prepare_unit(n):
-            (nope_lo, nope_hi), (rope_lo, rope_hi) = UNITS[n]
-            regroup_nope(nope_lo, nope_hi, nc.vector.tensor_copy)
-            rotate(rope_lo, rope_hi)
-            quantise_g(n)
+        def rest_of_unit(n):
+            times_sin(n, 1)
+            times_cos(n)
+            regroup_nope(UNITS[n][0][0], UNITS[n][0][1], nc.vector.tensor_copy)
+            add_products(n)
 
         for c in range(X_CHUNKS_ON_SCALAR):
             regroup_x(c, nc.scalar.copy)
         build_tables()
-        prepare_unit(0)
+        times_sin(0, 0)
+        rest_of_unit(0)
+        quantise_g(0)
         quantise_x(0)
         for c in range(X_CHUNKS_ON_SCALAR, DIM // X_CHUNK):
             regroup_x(c, nc.vector.tensor_copy)
         for c in range(1, DIM // X_CHUNK):
             quantise_x(c)
+        times_sin(1, 0)
         for n in range(1, COL_TILES):
-            prepare_unit(n)
+            rest_of_unit(n)
+            if n + 1 < COL_TILES:
+                times_sin(n + 1, 0)
+            quantise_g(n)
 
         for first_m, count_m, first_n, count_n, vector_too in SWEEPS:
             first_col = first_n * N_TILE

@@ -43,11 +43,11 @@ UNITS = (
 )
 SWEEPS = (
     (0, 12, 0, 1, False),
-    (0, 6, 1, 1, False),
-    (6, 6, 1, 2, False),
-    (0, 6, 2, 2, False),
-    (6, 6, 3, 3, True),
-    (0, 6, 4, 2, True),
+    (0, 7, 1, 1, False),
+    (7, 5, 1, 2, False),
+    (0, 7, 2, 2, False),
+    (7, 5, 3, 3, True),
+    (0, 7, 4, 2, True),
 )
 MOST_TILES = 3
 MOST_HEADS = 3

@@ -42,7 +42,7 @@ UNITS = (
     ((14, 16), (13, 16)),
 )
 SWEEPS = (
-    (0, 12, 0, 1, False),
+    (6, 6, 0, 1, False),
     (0, 7, 1, 1, False),
     (7, 5, 1, 2, False),
     (0, 7, 2, 2, False),
@@ -189,28 +189,10 @@ def tile_mla_pb_kernel(tc, x, wq_w, wq_b, cos, sin, grad_out, out):
         def rest_of_unit(n):
             times_sin(n, 1)
             times_cos(n)
-            regroup_nope(UNITS[n][0][0], UNITS[n][0][1], nc.vector.tensor_copy)
+            regroup_nope(UNITS[n][0][0] + (1 if n == 1 else 0), UNITS[n][0][1], nc.vector.tensor_copy)
             add_products(n)
 
-        for c in range(X_CHUNKS_ON_SCALAR):
-            regroup_x(c, nc.scalar.copy)
-        build_tables()
-        times_sin(0, 0)
-        rest_of_unit(0)
-        quantise_g(0)
-        quantise_x(0)
-        for c in range(X_CHUNKS_ON_SCALAR, DIM // X_CHUNK):
-            regroup_x(c, nc.vector.tensor_copy)
-        for c in range(1, DIM // X_CHUNK):
-            quantise_x(c)
-        times_sin(1, 0)
-        for n in range(1, COL_TILES):
-            rest_of_unit(n)
-            if n + 1 < COL_TILES:
-                times_sin(n + 1, 0)
-            quantise_g(n)
-
-        for first_m, count_m, first_n, count_n, vector_too in SWEEPS:
+        def sweep(first_m, count_m, first_n, count_n, vector_too):
             first_col = first_n * N_TILE
             width = count_n * N_TILE
             for m in range(first_m, first_m + count_m):
@@ -234,3 +216,26 @@ def tile_mla_pb_kernel(tc, x, wq_w, wq_b, cos, sin, grad_out, out):
                     else:
                         nc.scalar.copy(out=part, in_=acc[:])
                 nc.sync.dma_start(out=out[m_cols, first_col : first_col + width], in_=rows[:, 0:width])
+
+        for c in range(X_CHUNKS_ON_SCALAR):
+            regroup_x(c, nc.scalar.copy)
+        build_tables()
+        times_sin(0, 0)
+        rest_of_unit(0)
+        quantise_g(0)
+        quantise_x(0)
+        for c in range(X_CHUNKS_ON_SCALAR, DIM // X_CHUNK):
+            regroup_x(c, nc.vector.tensor_copy)
+        for c in range(1, DIM // X_CHUNK):
+            quantise_x(c)
+        times_sin(1, 0)
+        sweep(0, ROW_TILES // 2, 0, 1, False)
+        regroup_nope(UNITS[1][0][0], UNITS[1][0][0] + 1, nc.scalar.copy)
+        for n in range(1, COL_TILES):
+            rest_of_unit(n)
+            if n + 1 < COL_TILES:
+                times_sin(n + 1, 0)
+            quantise_g(n)
+
+        for first_m, count_m, first_n, count_n, vector_too in SWEEPS:
+            sweep(first_m, count_m, first_n, count_n, vector_too)

@@ -27,7 +27,7 @@ N_TILE = 512
 ROW_TILES = DIM // M_TILE
 COL_TILES = COLS // N_TILE
 X_CHUNK = 512
-RUN = 4
+RUN = 8
 
 FLOPS = 2 * TOKENS * DIM * COLS
 BYTES = 2 * TOKENS * DIM + 2 * TOKENS * COLS + 2 * 2 * SEQ * HALF + 4 * DIM * COLS

@@ -1,6 +1,7 @@
 from contextlib import ExitStack
 
 import concourse.mybir as mybir
+from concourse.masks import make_identity
 
 BF16 = mybir.dt.bfloat16
 F32 = mybir.dt.float32
@@ -64,7 +65,8 @@ def tile_mla_pb_kernel(tc, x, wq_w, wq_b, cos, sin, grad_out, out):
         keep = ctx.enter_context(tc.tile_pool(name="keep", bufs=1))
         products = ctx.enter_context(tc.tile_pool(name="products", bufs=2))
         stage = ctx.enter_context(tc.tile_pool(name="stage", bufs=8))
-        psum = ctx.enter_context(tc.psum_pool(name="psum", bufs=8))
+        psum = ctx.enter_context(tc.psum_pool(name="psum", bufs=7))
+        fixed = ctx.enter_context(tc.psum_pool(name="fixed", bufs=1))
         ctx.enter_context(tc.manual_schedule())
 
         trig = keep.tile([P, 2, PACK, HALF], BF16, name="trig")
@@ -99,18 +101,26 @@ def tile_mla_pb_kernel(tc, x, wq_w, wq_b, cos, sin, grad_out, out):
             assert shift + width <= HEAD
             return by_head[:, :, start // HEAD : start // HEAD + heads, shift : shift + width]
 
-        cos_table = keep.tile([P, ROPE, PACK], BF16, name="cos_table")
-        sin_table = keep.tile([P, HALF, 2, PACK], BF16, name="sin_table")
+        identity = keep.tile([P, P], BF16, name="identity")
+        make_identity(nc, identity[:])
+        tables = keep.tile([P, 2 * ROPE * PACK], BF16, name="tables")
+        cos_table = tables[:, 0 : ROPE * PACK].rearrange("p (c t) -> p c t", t=PACK)
+        sin_table = tables[:, ROPE * PACK : 2 * ROPE * PACK].rearrange("p (f e t) -> p f e t", e=2, t=PACK)
+        tables_ps = fixed.tile([P, 2 * ROPE * PACK], F32, name="tables_ps")
+        cos_ps = tables_ps[:, 0 : ROPE * PACK].rearrange("p (c t) -> p c t", t=PACK)
+        sin_ps = tables_ps[:, ROPE * PACK : 2 * ROPE * PACK].rearrange("p (f e t) -> p f e t", e=2, t=PACK)
+        gates = keep.tile([P, COL_TILES], F32, name="gates")
 
         def build_tables():
             cos_by_pair = trig[:, 0].rearrange("p t f -> p f t")
             sin_by_pair = trig[:, 1].rearrange("p t f -> p f t")
             for e in range(2):
                 nc.vector.tensor_copy(
-                    out=cos_table[:].rearrange("p (f e) t -> p f e t", e=2)[:, :, e, :], in_=cos_by_pair
+                    out=cos_table.rearrange("p (f e) t -> p f e t", e=2)[:, :, e, :], in_=cos_by_pair
                 )
             nc.vector.tensor_copy(out=sin_table[:, :, 0, :], in_=sin_by_pair)
             nc.vector.tensor_scalar_mul(out=sin_table[:, :, 1, :], in0=sin_by_pair, scalar1=-1.0)
+            nc.tensor.matmul(out=tables_ps[:], lhsT=identity[:], rhs=tables[:], start=True, stop=True)
 
         grouped_x = [
             keep.tile([P, X_CHUNK, PACK], BF16, name="grouped_x%d" % c, align_bytes=64)
@@ -145,6 +155,17 @@ def tile_mla_pb_kernel(tc, x, wq_w, wq_b, cos, sin, grad_out, out):
                 in_=raw_stretch(lo, hi - lo, 0, NOPE).rearrange("p t h (w i) -> p h w t i", i=RUN),
             )
 
+        def regroup_nope_on_gpsimd(n, lo, hi):
+            nc.vector.memset(gates[:, n : n + 1], 1.0)
+            nc.gpsimd.tensor_scalar(
+                out=grouped_heads[:, lo:hi, 0:NOPE, :],
+                in0=raw_stretch(lo, hi - lo, 0, NOPE).rearrange("p t h c -> p h c t"),
+                scalar1=gates[:, n : n + 1],
+                scalar2=0.0,
+                op0=MULT,
+                op1=ADD,
+            )
+
         by_cos = {}
         by_sin = {}
 
@@ -155,7 +176,7 @@ def tile_mla_pb_kernel(tc, x, wq_w, wq_b, cos, sin, grad_out, out):
             nc.vector.tensor_tensor(
                 out=by_sin[n][:, 0 : hi - lo].rearrange("p h (f e) t -> p h f e t", e=2)[:, :, :, e, :],
                 in0=raw_stretch(lo, hi - lo, NOPE, ROPE).rearrange("p t h (f e) -> p h f e t", e=2)[:, :, :, 1 - e, :],
-                in1=sin_table[:, :, e, :].unsqueeze(1).to_broadcast([P, hi - lo, HALF, PACK]),
+                in1=sin_ps[:, :, e, :].unsqueeze(1).to_broadcast([P, hi - lo, HALF, PACK]),
                 op=MULT,
             )
 
@@ -165,7 +186,7 @@ def tile_mla_pb_kernel(tc, x, wq_w, wq_b, cos, sin, grad_out, out):
             nc.vector.tensor_tensor(
                 out=by_cos[n][:, 0 : hi - lo],
                 in0=raw_stretch(lo, hi - lo, NOPE, ROPE).rearrange("p t h c -> p h c t"),
-                in1=cos_table[:].unsqueeze(1).to_broadcast([P, hi - lo, ROPE, PACK]),
+                in1=cos_ps.unsqueeze(1).to_broadcast([P, hi - lo, ROPE, PACK]),
                 op=MULT,
             )
 
@@ -186,11 +207,16 @@ def tile_mla_pb_kernel(tc, x, wq_w, wq_b, cos, sin, grad_out, out):
                 in_=grouped_g[:, cols, :].rearrange("p w t -> p (w t)"),
             )
 
-        def rest_of_unit(n):
+        def unit(n):
+            first = UNITS[n][0][0] + (1 if n == 1 else 0)
+            regroup_nope_on_gpsimd(n, first, first + 2)
+            times_sin(n, 0)
             times_sin(n, 1)
             times_cos(n)
-            regroup_nope(UNITS[n][0][0] + (1 if n == 1 else 0), UNITS[n][0][1], nc.vector.tensor_copy)
+            if first + 2 < UNITS[n][0][1]:
+                regroup_nope(first + 2, UNITS[n][0][1], nc.vector.tensor_copy)
             add_products(n)
+            quantise_g(n)
 
         def sweep(first_m, count_m, first_n, count_n, vector_too):
             first_col = first_n * N_TILE
@@ -220,22 +246,16 @@ def tile_mla_pb_kernel(tc, x, wq_w, wq_b, cos, sin, grad_out, out):
         for c in range(X_CHUNKS_ON_SCALAR):
             regroup_x(c, nc.scalar.copy)
         build_tables()
-        times_sin(0, 0)
-        rest_of_unit(0)
-        quantise_g(0)
+        unit(0)
         quantise_x(0)
         for c in range(X_CHUNKS_ON_SCALAR, DIM // X_CHUNK):
             regroup_x(c, nc.vector.tensor_copy)
         for c in range(1, DIM // X_CHUNK):
             quantise_x(c)
-        times_sin(1, 0)
         sweep(0, ROW_TILES // 2, 0, 1, False)
         regroup_nope(UNITS[1][0][0], UNITS[1][0][0] + 1, nc.scalar.copy)
         for n in range(1, COL_TILES):
-            rest_of_unit(n)
-            if n + 1 < COL_TILES:
-                times_sin(n + 1, 0)
-            quantise_g(n)
+            unit(n)
 
         for first_m, count_m, first_n, count_n, vector_too in SWEEPS:
             sweep(first_m, count_m, first_n, count_n, vector_too)

@@ -43,14 +43,14 @@ UNITS = (
     ((14, 16), (13, 16)),
 )
 SWEEPS = (
-    (6, 6, 0, 1, False),
-    (0, 7, 1, 1, False),
-    (7, 5, 1, 2, False),
-    (0, 7, 2, 2, False),
-    (7, 5, 3, 3, True),
-    (0, 7, 4, 2, True),
+    (0, 6, 1, 1, False),
+    (6, 6, 1, 2, False),
+    (0, 3, 2, 2, False),
+    (6, 6, 3, 3, True),
+    (3, 3, 2, 4, True),
+    (0, 3, 4, 2, True),
 )
-MOST_TILES = 3
+MOST_TILES = 4
 MOST_HEADS = 3
 X_CHUNKS_ON_SCALAR = 2
 
@@ -208,7 +208,7 @@ def tile_mla_pb_kernel(tc, x, wq_w, wq_b, cos, sin, grad_out, out):
             )
 
         def unit(n):
-            first = UNITS[n][0][0] + (1 if n == 1 else 0)
+            first = UNITS[n][0][0]
             regroup_nope_on_gpsimd(n, first, first + 2)
             times_sin(n, 0)
             times_sin(n, 1)
@@ -218,6 +218,7 @@ def tile_mla_pb_kernel(tc, x, wq_w, wq_b, cos, sin, grad_out, out):
             add_products(n)
             quantise_g(n)
 
+        turns = []
         def sweep(first_m, count_m, first_n, count_n, vector_too):
             first_col = first_n * N_TILE
             width = count_n * N_TILE
@@ -237,7 +238,9 @@ def tile_mla_pb_kernel(tc, x, wq_w, wq_b, cos, sin, grad_out, out):
                         stop=True,
                     )
                     part = rows[:, i * N_TILE : (i + 1) * N_TILE]
-                    if vector_too and i % 2 == 1:
+                    if vector_too:
+                        turns.append(m)
+                    if vector_too and len(turns) % 2 == 0:
                         nc.vector.tensor_copy(out=part, in_=acc[:])
                     else:
                         nc.scalar.copy(out=part, in_=acc[:])
@@ -252,8 +255,7 @@ def tile_mla_pb_kernel(tc, x, wq_w, wq_b, cos, sin, grad_out, out):
             regroup_x(c, nc.vector.tensor_copy)
         for c in range(1, DIM // X_CHUNK):
             quantise_x(c)
-        sweep(0, ROW_TILES // 2, 0, 1, False)
-        regroup_nope(UNITS[1][0][0], UNITS[1][0][0] + 1, nc.scalar.copy)
+        sweep(0, ROW_TILES, 0, 1, False)
         for n in range(1, COL_TILES):
             unit(n)
 

@@ -180,22 +180,30 @@ def tile_mla_pb_kernel(tc, x, wq_w, wq_b, cos, sin, grad_out, out):
                 op=MULT,
             )
 
-        def times_cos(n):
+        def halves(n):
             lo, hi = UNITS[n][1]
-            by_cos[n] = products.tile([P, MOST_HEADS, ROPE, PACK], F32, name="by_cos")
+            mid = (lo + hi + 1) // 2
+            return ((lo, mid), (mid, hi))
+
+        def times_cos(n, part):
+            lo = UNITS[n][1][0]
+            a, b = halves(n)[part]
+            if part == 0:
+                by_cos[n] = products.tile([P, MOST_HEADS, ROPE, PACK], F32, name="by_cos")
             nc.vector.tensor_tensor(
-                out=by_cos[n][:, 0 : hi - lo],
-                in0=raw_stretch(lo, hi - lo, NOPE, ROPE).rearrange("p t h c -> p h c t"),
-                in1=cos_ps.unsqueeze(1).to_broadcast([P, hi - lo, ROPE, PACK]),
+                out=by_cos[n][:, a - lo : b - lo],
+                in0=raw_stretch(a, b - a, NOPE, ROPE).rearrange("p t h c -> p h c t"),
+                in1=cos_ps.unsqueeze(1).to_broadcast([P, b - a, ROPE, PACK]),
                 op=MULT,
             )
 
-        def add_products(n):
-            lo, hi = UNITS[n][1]
+        def add_products(n, part):
+            lo = UNITS[n][1][0]
+            a, b = halves(n)[part]
             nc.vector.tensor_tensor(
-                out=grouped_heads[:, lo:hi, NOPE:HEAD, :],
-                in0=by_cos[n][:, 0 : hi - lo],
-                in1=by_sin[n][:, 0 : hi - lo],
+                out=grouped_heads[:, a:b, NOPE:HEAD, :],
+                in0=by_cos[n][:, a - lo : b - lo],
+                in1=by_sin[n][:, a - lo : b - lo],
                 op=ADD,
             )
 
@@ -210,12 +218,15 @@ def tile_mla_pb_kernel(tc, x, wq_w, wq_b, cos, sin, grad_out, out):
         def unit(n):
             first = UNITS[n][0][0]
             regroup_nope_on_gpsimd(n, first, first + 2)
-            times_sin(n, 0)
             times_sin(n, 1)
-            times_cos(n)
+            times_cos(n, 0)
+            times_cos(n, 1)
             if first + 2 < UNITS[n][0][1]:
                 regroup_nope(first + 2, UNITS[n][0][1], nc.vector.tensor_copy)
-            add_products(n)
+            add_products(n, 0)
+            add_products(n, 1)
+            if 0 < n < COL_TILES - 1:
+                times_sin(n + 1, 0)
             quantise_g(n)
 
         turns = []
@@ -249,12 +260,14 @@ def tile_mla_pb_kernel(tc, x, wq_w, wq_b, cos, sin, grad_out, out):
         for c in range(X_CHUNKS_ON_SCALAR):
             regroup_x(c, nc.scalar.copy)
         build_tables()
+        times_sin(0, 0)
         unit(0)
         quantise_x(0)
         for c in range(X_CHUNKS_ON_SCALAR, DIM // X_CHUNK):
             regroup_x(c, nc.vector.tensor_copy)
         for c in range(1, DIM // X_CHUNK):
             quantise_x(c)
+        times_sin(1, 0)
         sweep(0, ROW_TILES, 0, 1, False)
         for n in range(1, COL_TILES):
             unit(n)

@@ -76,11 +76,11 @@ def tile_mla_pb_kernel(tc, x, wq_w, wq_b, cos, sin, grad_out, out):
             nc.sync.dma_start(out=trig[rows, 1], in_=sin.rearrange("(p t) f -> p t f", t=PACK))
 
         raw_g = [
-            keep.tile([P, PACK, -(-width // HEAD) * HEAD], BF16, name="raw_g%d" % k)
+            keep.tile([P, PACK, -(-width // HEAD) * HEAD], BF16, name="raw_g%d" % k, align_bytes=256)
             for k, (first, width) in enumerate(G_LOADS)
         ]
-        raw_x0 = keep.tile([P, PACK, X_CHUNK], BF16, name="raw_x0")
-        raw_x1 = keep.tile([P, PACK, DIM - X_CHUNK], BF16, name="raw_x1")
+        raw_x0 = keep.tile([P, PACK, X_CHUNK], BF16, name="raw_x0", align_bytes=256)
+        raw_x1 = keep.tile([P, PACK, DIM - X_CHUNK], BF16, name="raw_x1", align_bytes=256)
 
         def load_g(k):
             first, width = G_LOADS[k]
@@ -235,7 +235,7 @@ def tile_mla_pb_kernel(tc, x, wq_w, wq_b, cos, sin, grad_out, out):
             width = count_n * N_TILE
             for m in range(first_m, first_m + count_m):
                 m_cols = slice(m * M_TILE, (m + 1) * M_TILE)
-                rows = stage.tile([P, MOST_TILES * N_TILE], F32, name="rows")
+                rows = stage.tile([P, MOST_TILES * N_TILE], F32, name="rows", align_bytes=256)
                 for i in range(count_n):
                     n_cols = slice(first_col + i * N_TILE, first_col + (i + 1) * N_TILE)
                     acc = psum.tile([M_TILE, N_TILE], F32, name="acc")

@@ -52,7 +52,7 @@ SWEEPS = (
 )
 MOST_TILES = 4
 MOST_HEADS = 3
-X_CHUNKS_ON_SCALAR = 2
+X_CHUNKS_ON_SCALAR = (0, 2)
 
 
 def tile_mla_pb_kernel(tc, x, wq_w, wq_b, cos, sin, grad_out, out):
@@ -69,14 +69,14 @@ def tile_mla_pb_kernel(tc, x, wq_w, wq_b, cos, sin, grad_out, out):
         fixed = ctx.enter_context(tc.psum_pool(name="fixed", bufs=1))
         ctx.enter_context(tc.manual_schedule())
 
-        trig = keep.tile([P, 2, PACK, HALF], BF16, name="trig")
+        trig = keep.tile([P, 2, PACK, HALF], BF16, name="trig", align_bytes=256)
         for half in range(TOKENS // SEQ):
             rows = slice(half * (SEQ // PACK), (half + 1) * (SEQ // PACK))
             nc.sync.dma_start(out=trig[rows, 0], in_=cos.rearrange("(p t) f -> p t f", t=PACK))
             nc.sync.dma_start(out=trig[rows, 1], in_=sin.rearrange("(p t) f -> p t f", t=PACK))
 
         raw_g = [
-            keep.tile([P, PACK, -(-width // HEAD) * HEAD], BF16, name="raw_g%d" % k, align_bytes=256)
+            keep.tile([P, PACK, -(-width // (2 * HEAD)) * 2 * HEAD], BF16, name="raw_g%d" % k, align_bytes=256)
             for k, (first, width) in enumerate(G_LOADS)
         ]
         raw_x0 = keep.tile([P, PACK, X_CHUNK], BF16, name="raw_x0", align_bytes=256)
@@ -207,8 +207,8 @@ def tile_mla_pb_kernel(tc, x, wq_w, wq_b, cos, sin, grad_out, out):
                 op=ADD,
             )
 
-        def quantise_g(n):
-            cols = slice(n * N_TILE, (n + 1) * N_TILE)
+        def quantise_g(n, first=0, count=N_TILE):
+            cols = slice(n * N_TILE + first, n * N_TILE + first + count)
             nc.vector.quantize_mx(
                 out=g_codes[:, cols].bitcast(E5M2_X4),
                 scales=g_scales[:, cols],
@@ -227,7 +227,10 @@ def tile_mla_pb_kernel(tc, x, wq_w, wq_b, cos, sin, grad_out, out):
             add_products(n, 1)
             if 0 < n < COL_TILES - 1:
                 times_sin(n + 1, 0)
-            quantise_g(n)
+                quantise_g(n)
+            else:
+                quantise_g(n, 0, N_TILE // 2)
+                quantise_g(n, N_TILE // 2, N_TILE // 2)
 
         turns = []
         def sweep(first_m, count_m, first_n, count_n, vector_too):
@@ -257,15 +260,13 @@ def tile_mla_pb_kernel(tc, x, wq_w, wq_b, cos, sin, grad_out, out):
                         nc.scalar.copy(out=part, in_=acc[:])
                 nc.sync.dma_start(out=out[m_cols, first_col : first_col + width], in_=rows[:, 0:width])
 
-        for c in range(X_CHUNKS_ON_SCALAR):
+        for c in X_CHUNKS_ON_SCALAR:
             regroup_x(c, nc.scalar.copy)
         build_tables()
         times_sin(0, 0)
         unit(0)
-        quantise_x(0)
-        for c in range(X_CHUNKS_ON_SCALAR, DIM // X_CHUNK):
-            regroup_x(c, nc.vector.tensor_copy)
-        for c in range(1, DIM // X_CHUNK):
+        regroup_x(1, nc.vector.tensor_copy)
+        for c in range(DIM // X_CHUNK):
             quantise_x(c)
         times_sin(1, 0)
         sweep(0, ROW_TILES, 0, 1, False)

@@ -218,6 +218,7 @@ def tile_mla_pb_kernel(tc, x, wq_w, wq_b, cos, sin, grad_out, out):
         def unit(n):
             first = UNITS[n][0][0]
             regroup_nope_on_gpsimd(n, first, first + 2)
+            times_sin(n, 0)
             times_sin(n, 1)
             times_cos(n, 0)
             times_cos(n, 1)
@@ -225,12 +226,8 @@ def tile_mla_pb_kernel(tc, x, wq_w, wq_b, cos, sin, grad_out, out):
                 regroup_nope(first + 2, UNITS[n][0][1], nc.vector.tensor_copy)
             add_products(n, 0)
             add_products(n, 1)
-            if 0 < n < COL_TILES - 1:
-                times_sin(n + 1, 0)
-                quantise_g(n)
-            else:
-                quantise_g(n, 0, N_TILE // 2)
-                quantise_g(n, N_TILE // 2, N_TILE // 2)
+            quantise_g(n, 0, N_TILE // 2)
+            quantise_g(n, N_TILE // 2, N_TILE // 2)
 
         turns = []
         def sweep(first_m, count_m, first_n, count_n, vector_too):
@@ -263,12 +260,10 @@ def tile_mla_pb_kernel(tc, x, wq_w, wq_b, cos, sin, grad_out, out):
         for c in X_CHUNKS_ON_SCALAR:
             regroup_x(c, nc.scalar.copy)
         build_tables()
-        times_sin(0, 0)
         unit(0)
         regroup_x(1, nc.vector.tensor_copy)
         for c in range(DIM // X_CHUNK):
             quantise_x(c)
-        times_sin(1, 0)
         sweep(0, ROW_TILES, 0, 1, False)
         for n in range(1, COL_TILES):
             unit(n)

from contextlib import ExitStack

import concourse.mybir as mybir
from concourse.masks import make_identity

BF16 = mybir.dt.bfloat16
F32 = mybir.dt.float32
U32 = mybir.dt.uint32
U8 = mybir.dt.uint8
E4M3_X4 = mybir.dt.float8_e4m3fn_x4
E5M2_X4 = mybir.dt.float8_e5m2_x4
MULT = mybir.AluOpType.mult
ADD = mybir.AluOpType.add

P = 128
PACK = 4
TOKENS = P * PACK
SEQ = 256
DIM = 1536
HEADS = 16
NOPE = 128
ROPE = 64
HALF = ROPE // 2
HEAD = NOPE + ROPE
COLS = HEADS * HEAD
M_TILE = 128
N_TILE = 512
ROW_TILES = DIM // M_TILE
COL_TILES = COLS // N_TILE
X_CHUNK = 512
RUN = 8

FLOPS = 2 * TOKENS * DIM * COLS
BYTES = 2 * TOKENS * DIM + 2 * TOKENS * COLS + 2 * 2 * SEQ * HALF + 4 * DIM * COLS

G_LOADS = ((0, 512), (512, 1024), (1536, 1536))
UNITS = (
    ((0, 3), (0, 2)),
    ((3, 6), (2, 5)),
    ((6, 8), (5, 8)),
    ((8, 11), (8, 10)),
    ((11, 14), (10, 13)),
    ((14, 16), (13, 16)),
)
SWEEPS = (
    (0, 6, 1, 1, False),
    (6, 6, 1, 2, False),
    (0, 3, 2, 2, False),
    (6, 6, 3, 3, True),
    (3, 3, 2, 4, True),
    (0, 3, 4, 2, True),
)
MOST_TILES = 4
MOST_HEADS = 3
X_CHUNKS_ON_SCALAR = (0, 2)


def tile_mla_pb_kernel(tc, x, wq_w, wq_b, cos, sin, grad_out, out):
    nc = tc.nc

    x_rows = x.rearrange("b s d -> (b s) d").rearrange("(p t) d -> p t d", t=PACK)
    g_rows = grad_out.rearrange("b s h c -> (b s) (h c)").rearrange("(p t) c -> p t c", t=PACK)

    with ExitStack() as ctx:
        keep = ctx.enter_context(tc.tile_pool(name="keep", bufs=1))
        products = ctx.enter_context(tc.tile_pool(name="products", bufs=2))
        stage = ctx.enter_context(tc.tile_pool(name="stage", bufs=8))
        psum = ctx.enter_context(tc.psum_pool(name="psum", bufs=7))
        fixed = ctx.enter_context(tc.psum_pool(name="fixed", bufs=1))
        ctx.enter_context(tc.manual_schedule())

        trig = keep.tile([P, 2, PACK, HALF], BF16, name="trig", align_bytes=256)
        for half in range(TOKENS // SEQ):
            rows = slice(half * (SEQ // PACK), (half + 1) * (SEQ // PACK))
            nc.sync.dma_start(out=trig[rows, 0], in_=cos.rearrange("(p t) f -> p t f", t=PACK))
            nc.sync.dma_start(out=trig[rows, 1], in_=sin.rearrange("(p t) f -> p t f", t=PACK))

        raw_g = [
            keep.tile([P, PACK, -(-width // (2 * HEAD)) * 2 * HEAD], BF16, name="raw_g%d" % k, align_bytes=256)
            for k, (first, width) in enumerate(G_LOADS)
        ]
        raw_x0 = keep.tile([P, PACK, X_CHUNK], BF16, name="raw_x0", align_bytes=256)
        raw_x1 = keep.tile([P, PACK, DIM - X_CHUNK], BF16, name="raw_x1", align_bytes=256)

        def load_g(k):
            first, width = G_LOADS[k]
            nc.sync.dma_start(out=raw_g[k][:, :, 0:width], in_=g_rows[:, :, first : first + width])

        load_g(0)
        nc.sync.dma_start(out=raw_x0[:], in_=x_rows[:, :, 0:X_CHUNK])
        nc.sync.dma_start(out=raw_x1[:], in_=x_rows[:, :, X_CHUNK:DIM])
        load_g(1)
        load_g(2)

        def raw_stretch(first_head, heads, offset, width):
            col = first_head * HEAD + offset
            k = max(i for i, (first, w) in enumerate(G_LOADS) if first <= col)
            start = col - G_LOADS[k][0]
            shift = start % HEAD
            by_head = raw_g[k][:].rearrange("p t (h c) -> p t h c", c=HEAD)
            assert shift + width <= HEAD
            return by_head[:, :, start // HEAD : start // HEAD + heads, shift : shift + width]

        identity = keep.tile([P, P], BF16, name="identity")
        make_identity(nc, identity[:])
        tables = keep.tile([P, 2 * ROPE * PACK], BF16, name="tables")
        cos_table = tables[:, 0 : ROPE * PACK].rearrange("p (c t) -> p c t", t=PACK)
        sin_table = tables[:, ROPE * PACK : 2 * ROPE * PACK].rearrange("p (f e t) -> p f e t", e=2, t=PACK)
        tables_ps = fixed.tile([P, 2 * ROPE * PACK], F32, name="tables_ps")
        cos_ps = tables_ps[:, 0 : ROPE * PACK].rearrange("p (c t) -> p c t", t=PACK)
        sin_ps = tables_ps[:, ROPE * PACK : 2 * ROPE * PACK].rearrange("p (f e t) -> p f e t", e=2, t=PACK)
        gates = keep.tile([P, COL_TILES], F32, name="gates")

        def build_tables():
            cos_by_pair = trig[:, 0].rearrange("p t f -> p f t")
            sin_by_pair = trig[:, 1].rearrange("p t f -> p f t")
            for e in range(2):
                nc.vector.tensor_copy(
                    out=cos_table.rearrange("p (f e) t -> p f e t", e=2)[:, :, e, :], in_=cos_by_pair
                )
            nc.vector.tensor_copy(out=sin_table[:, :, 0, :], in_=sin_by_pair)
            nc.vector.tensor_scalar_mul(out=sin_table[:, :, 1, :], in0=sin_by_pair, scalar1=-1.0)
            nc.tensor.matmul(out=tables_ps[:], lhsT=identity[:], rhs=tables[:], start=True, stop=True)

        grouped_x = [
            keep.tile([P, X_CHUNK, PACK], BF16, name="grouped_x%d" % c, align_bytes=64)
            for c in range(DIM // X_CHUNK)
        ]
        grouped_g = keep.tile([P, COLS, PACK], BF16, name="grouped_g", align_bytes=64)
        x_codes = keep.tile([P, DIM], U32, name="x_codes", align_bytes=64)
        x_scales = keep.tile([P, DIM], U8, name="x_scales", align_bytes=64)
        g_codes = keep.tile([P, COLS], U32, name="g_codes", align_bytes=64)
        g_scales = keep.tile([P, COLS], U8, name="g_scales", align_bytes=64)

        def regroup_x(c, copy):
            raw = raw_x0[:] if c == 0 else raw_x1[:, :, (c - 1) * X_CHUNK : c * X_CHUNK]
            copy(
                out=grouped_x[c][:].rearrange("p (w i) t -> p w t i", i=RUN),
                in_=raw.rearrange("p t (w i) -> p w t i", i=RUN),
            )

        def quantise_x(c):
            cols = slice(c * X_CHUNK, (c + 1) * X_CHUNK)
            nc.vector.quantize_mx(
                out=x_codes[:, cols].bitcast(E4M3_X4),
                scales=x_scales[:, cols],
                in_=grouped_x[c][:].rearrange("p w t -> p (w t)"),
            )

        grouped_heads = grouped_g[:].rearrange("p (h c) t -> p h c t", c=HEAD)

        def regroup_nope(lo, hi, copy):
            copy(
                out=grouped_heads[:, lo:hi, 0:NOPE, :].rearrange("p h (w i) t -> p h w t i", i=RUN),
                in_=raw_stretch(lo, hi - lo, 0, NOPE).rearrange("p t h (w i) -> p h w t i", i=RUN),
            )

        def regroup_nope_on_gpsimd(n, lo, hi):
            nc.vector.memset(gates[:, n : n + 1], 1.0)
            nc.gpsimd.tensor_scalar(
                out=grouped_heads[:, lo:hi, 0:NOPE, :],
                in0=raw_stretch(lo, hi - lo, 0, NOPE).rearrange("p t h c -> p h c t"),
                scalar1=gates[:, n : n + 1],
                scalar2=0.0,
                op0=MULT,
                op1=ADD,
            )

        by_cos = {}
        by_sin = {}

        def times_sin(n, e):
            lo, hi = UNITS[n][1]
            if e == 0:
                by_sin[n] = products.tile([P, MOST_HEADS, ROPE, PACK], F32, name="by_sin")
            nc.vector.tensor_tensor(
                out=by_sin[n][:, 0 : hi - lo].rearrange("p h (f e) t -> p h f e t", e=2)[:, :, :, e, :],
                in0=raw_stretch(lo, hi - lo, NOPE, ROPE).rearrange("p t h (f e) -> p h f e t", e=2)[:, :, :, 1 - e, :],
                in1=sin_ps[:, :, e, :].unsqueeze(1).to_broadcast([P, hi - lo, HALF, PACK]),
                op=MULT,
            )

        def halves(n):
            lo, hi = UNITS[n][1]
            mid = (lo + hi + 1) // 2
            return ((lo, mid), (mid, hi))

        def times_cos(n, part):
            lo = UNITS[n][1][0]
            a, b = halves(n)[part]
            if part == 0:
                by_cos[n] = products.tile([P, MOST_HEADS, ROPE, PACK], F32, name="by_cos")
            nc.vector.tensor_tensor(
                out=by_cos[n][:, a - lo : b - lo],
                in0=raw_stretch(a, b - a, NOPE, ROPE).rearrange("p t h c -> p h c t"),
                in1=cos_ps.unsqueeze(1).to_broadcast([P, b - a, ROPE, PACK]),
                op=MULT,
            )

        def add_products(n, part):
            lo = UNITS[n][1][0]
            a, b = halves(n)[part]
            nc.vector.tensor_tensor(
                out=grouped_heads[:, a:b, NOPE:HEAD, :],
                in0=by_cos[n][:, a - lo : b - lo],
                in1=by_sin[n][:, a - lo : b - lo],
                op=ADD,
            )

        def quantise_g(n, first=0, count=N_TILE):
            cols = slice(n * N_TILE + first, n * N_TILE + first + count)
            nc.vector.quantize_mx(
                out=g_codes[:, cols].bitcast(E5M2_X4),
                scales=g_scales[:, cols],
                in_=grouped_g[:, cols, :].rearrange("p w t -> p (w t)"),
            )

        def unit(n):
            first = UNITS[n][0][0]
            regroup_nope_on_gpsimd(n, first, first + 2)
            times_sin(n, 0)
            times_sin(n, 1)
            times_cos(n, 0)
            times_cos(n, 1)
            if first + 2 < UNITS[n][0][1]:
                regroup_nope(first + 2, UNITS[n][0][1], nc.vector.tensor_copy)
            add_products(n, 0)
            add_products(n, 1)
            quantise_g(n, 0, N_TILE // 2)
            quantise_g(n, N_TILE // 2, N_TILE // 2)

        turns = []
        def sweep(first_m, count_m, first_n, count_n, vector_too):
            first_col = first_n * N_TILE
            width = count_n * N_TILE
            for m in range(first_m, first_m + count_m):
                m_cols = slice(m * M_TILE, (m + 1) * M_TILE)
                rows = stage.tile([P, MOST_TILES * N_TILE], F32, name="rows", align_bytes=256)
                for i in range(count_n):
                    n_cols = slice(first_col + i * N_TILE, first_col + (i + 1) * N_TILE)
                    acc = psum.tile([M_TILE, N_TILE], F32, name="acc")
                    nc.tensor.matmul_mx(
                        out=acc[:],
                        lhsT=x_codes[:, m_cols].bitcast(E4M3_X4),
                        lhsT_scale=x_scales[:, m_cols],
                        rhs=g_codes[:, n_cols].bitcast(E5M2_X4),
                        rhs_scale=g_scales[:, n_cols],
                        start=True,
                        stop=True,
                    )
                    part = rows[:, i * N_TILE : (i + 1) * N_TILE]
                    if vector_too:
                        turns.append(m)
                    if vector_too and len(turns) % 2 == 0:
                        nc.vector.tensor_copy(out=part, in_=acc[:])
                    else:
                        nc.scalar.copy(out=part, in_=acc[:])
                nc.sync.dma_start(out=out[m_cols, first_col : first_col + width], in_=rows[:, 0:width])

        for c in X_CHUNKS_ON_SCALAR:
            regroup_x(c, nc.scalar.copy)
        build_tables()
        unit(0)
        regroup_x(1, nc.vector.tensor_copy)
        for c in range(DIM // X_CHUNK):
            quantise_x(c)
        sweep(0, ROW_TILES, 0, 1, False)
        for n in range(1, COL_TILES):
            unit(n)

        for first_m, count_m, first_n, count_n, vector_too in SWEEPS:
            sweep(first_m, count_m, first_n, count_n, vector_too)
